import numpy as np
import ml_dtypes


def mxq(x, axis, fmt="e4m3"):
    dtype, down = {"e4m3": (ml_dtypes.float8_e4m3fn, 7), "e5m2": (ml_dtypes.float8_e5m2, 14)}[fmt]
    v = np.moveaxis(np.asarray(x, np.float32).astype(ml_dtypes.bfloat16).astype(np.float64), axis, -1)
    blocks = v.reshape(v.shape[:-1] + (-1, 32))
    amax = np.abs(blocks).max(-1, keepdims=True)
    byte = np.maximum(np.where(amax > 0, np.frexp(amax)[1] - 1 + 127, 0) - down, 1)
    scale = np.exp2(byte - 127.0)
    codes = (blocks / scale).astype(np.float32).astype(dtype).astype(np.float64)
    return np.moveaxis((codes * scale).reshape(v.shape), -1, axis)


WIDE = False


def mx_kscale(k):
    if not WIDE:
        return np.ones(k)
    levels = np.array([10, -10, 5, -5, 0])
    a = np.random.permutation(np.resize(levels, k // 512 * 4)).reshape(k // 512, 4)
    idx = np.arange(k)
    return np.exp2(a[idx // 512, idx % 128 // 32])


BF16 = ml_dtypes.bfloat16


def bf(x):
    return np.asarray(x, np.float32).astype(BF16)


def f64(x):
    return np.asarray(x).astype(np.float64)


B, S, H, N, L = 2, 256, 512, 256, 10
EPS = 1e-06


def setup_inputs():
    s = mx_kscale(H)
    return {"hidden_states": bf(np.random.standard_normal((B, S, H)) * s),
            "conv_w": bf(np.random.standard_normal((L, N, H)) / np.sqrt(H) / s),
            "norm_w": bf(1.0 + 0.1 * np.random.standard_normal(N))}


def reference(hidden_states, conv_w, norm_w):
    x = f64(hidden_states)
    w_sum = f64(conv_w).sum(axis=0)
    out = (mxq(x, 2, "e4m3") @ mxq(w_sum, 1, "e4m3").T) / L
    norm_x = np.sqrt(np.sum(out * out, axis=-1, keepdims=True) + EPS * H)
    x_normed = out / norm_x * np.sqrt(H)
    return x_normed * f64(norm_w)

@@ -1,0 +1,170 @@
+import math
+
+import concourse.mybir as mybir
+from concourse.masks import make_identity
+
+BF16 = mybir.dt.bfloat16
+F32 = mybir.dt.float32
+U32 = mybir.dt.uint32
+U8 = mybir.dt.uint8
+FP8X4 = mybir.dt.float8_e4m3fn_x4
+ADD = mybir.AluOpType.add
+MULT = mybir.AluOpType.mult
+FUNC = mybir.ActivationFunctionType
+
+P = 128
+TOKENS = 512
+H = 512
+CHANNELS = 256
+LAYERS = 10
+EPS = 1e-06
+TOKEN_TILES = TOKENS // P
+CHANNEL_TILES = CHANNELS // P
+HALVES = 2
+PAIR = 2
+PACK = HALVES * PAIR
+
+X_BEHIND_LAYER = 2
+X_QUANTISED_BEHIND_LAYER = 4
+
+FLOPS = 2 * TOKENS * H * CHANNELS
+
+
+def tile_conv2dlinalgrmsnorm_s_kernel(tc, hidden_states, conv_w, norm_w, out):
+    nc = tc.nc
+    x_dram = hidden_states.flatten_outer_dims().rearrange("(p a) h -> p a h", a=TOKEN_TILES)
+    w_dram = conv_w.rearrange("l (p t) h -> l p t h", t=CHANNEL_TILES)
+    out_dram = out.flatten_outer_dims().rearrange("(p a) c -> p a c", a=TOKEN_TILES)
+
+    with (
+        tc.tile_pool(name="keep", bufs=1) as keep,
+        tc.tile_pool(name="layers", bufs=LAYERS) as layers,
+        tc.psum_pool(name="banks", bufs=8) as banks,
+    ):
+        ident = keep.tile([P, P], F32)
+        make_identity(nc, ident[:])
+        ones = keep.tile([P, P], BF16)
+        nc.vector.memset(ones[:], 1.0)
+        gain_row = keep.tile([P, CHANNELS], BF16)
+        nc.vector.memset(gain_row[:], 0.0)
+        warm = keep.tile([P, 1], F32)
+        nc.vector.memset(warm[:], 1.0)
+        nc.scalar.activation(out=warm[:], in_=warm[:], func=FUNC.Sqrt)
+
+        nc.scalar.dma_start(out=gain_row[0:1, :], in_=norm_w.unsqueeze(0))
+        w_sb = []
+        x_sb = keep.tile([P, TOKEN_TILES, H], BF16)
+        for l in range(LAYERS):
+            w_l = layers.tile([P, CHANNEL_TILES, H], BF16, tag="w")
+            nc.sync.dma_start(out=w_l[:], in_=w_dram[l])
+            w_sb.append(w_l)
+            if l == X_BEHIND_LAYER:
+                nc.sync.dma_start(out=x_sb[:], in_=x_dram)
+
+        gain_ps = banks.tile([P, CHANNELS], F32, tag="bank")
+        nc.tensor.matmul(out=gain_ps[:], lhsT=ones[:], rhs=gain_row[:], start=True, stop=True)
+        gain = keep.tile([P, CHANNELS], F32)
+        nc.scalar.activation(
+            out=gain[:], in_=gain_ps[:], func=FUNC.Copy, scale=math.sqrt(H) / LAYERS
+        )
+
+        def transposed_layer(l):
+            w_t = banks.tile([P, CHANNEL_TILES, HALVES, P], F32, tag="bank")
+            words = w_sb[l][:].bitcast(F32)
+            for t in range(CHANNEL_TILES):
+                for u in range(HALVES):
+                    nc.tensor.transpose(w_t[:, t, u, :], words[:, t, u * P : (u + 1) * P], ident[:])
+            return w_t
+
+        w_acc = keep.tile([P, CHANNEL_TILES, HALVES * P * PAIR], F32)
+        w_grouped = keep.tile([P, CHANNEL_TILES, P, PACK], BF16, align_bytes=64)
+        x_grouped = keep.tile([P, TOKEN_TILES, P, PACK], BF16, align_bytes=64)
+        x_codes = keep.tile([P, TOKENS], U32, align_bytes=64)
+        x_scales = keep.tile([P, TOKENS], U8, align_bytes=64)
+        w_codes = keep.tile([P, CHANNELS], U32, align_bytes=64)
+        w_scales = keep.tile([P, CHANNELS], U8, align_bytes=64)
+
+        for l in range(LAYERS):
+            w_t = transposed_layer(l)
+            for t in range(CHANNEL_TILES):
+                values = w_t[:, t].bitcast(BF16)
+                if l == 0:
+                    nc.scalar.copy(out=w_acc[:, t, :], in_=values.rearrange("q u c -> q (u c)"))
+                elif l < LAYERS - 1:
+                    nc.vector.tensor_tensor(
+                        out=w_acc[:, t, :],
+                        in0=values.rearrange("q u c -> q (u c)"),
+                        in1=w_acc[:, t, :],
+                        op=ADD,
+                    )
+                else:
+                    nc.vector.tensor_tensor(
+                        out=w_grouped[:, t].rearrange("q p (u e) -> q p u e", e=PAIR),
+                        in0=values.rearrange("q u (p e) -> q p u e", e=PAIR),
+                        in1=w_acc[:, t, :].rearrange("q (u p e) -> q p u e", u=HALVES, e=PAIR),
+                        op=ADD,
+                    )
+            if l == X_BEHIND_LAYER:
+                x_words = x_sb[:].bitcast(F32)
+                x_grouped_words = x_grouped[:].bitcast(F32)
+                for a0 in range(0, TOKEN_TILES, 2):
+                    x_t = banks.tile([P, 2, HALVES, P], F32, tag="bank")
+                    for a in range(2):
+                        for u in range(HALVES):
+                            nc.tensor.transpose(
+                                x_t[:, a, u, :], x_words[:, a0 + a, u * P : (u + 1) * P], ident[:]
+                            )
+                    nc.scalar.copy(
+                        out=x_grouped_words[:, a0 : a0 + 2],
+                        in_=x_t[:].rearrange("q a u r -> q a r u"),
+                    )
+            if l == X_QUANTISED_BEHIND_LAYER:
+                nc.vector.quantize_mx(
+                    out=x_codes[:].bitcast(FP8X4),
+                    scales=x_scales[:],
+                    in_=x_grouped[:].rearrange("q a r k -> q (a r k)"),
+                )
+
+        nc.vector.quantize_mx(
+            out=w_codes[:].bitcast(FP8X4),
+            scales=w_scales[:],
+            in_=w_grouped[:].rearrange("q t p k -> q (t p k)"),
+        )
+
+        squares = keep.tile([P, CHANNELS], F32)
+        sum_sq = keep.tile([P, TOKEN_TILES], F32)
+        norm = keep.tile([P, TOKEN_TILES], F32)
+        inv_norm = keep.tile([P, TOKEN_TILES], F32)
+        out_sb = keep.tile([P, TOKEN_TILES, CHANNELS], F32)
+        for a in range(TOKEN_TILES):
+            rows = slice(a * P, (a + 1) * P)
+            y = banks.tile([P, CHANNELS], F32, tag="bank")
+            nc.tensor.matmul_mx(
+                out=y[:],
+                lhsT=x_codes[:, rows].bitcast(FP8X4),
+                lhsT_scale=x_scales[:, rows],
+                rhs=w_codes[:].bitcast(FP8X4),
+                rhs_scale=w_scales[:],
+                start=True,
+                stop=True,
+            )
+            nc.scalar.activation(
+                out=squares[:],
+                in_=y[:],
+                func=FUNC.Square,
+                scale=1.0 / LAYERS,
+                accum_out=sum_sq[:, a : a + 1],
+            )
+            nc.scalar.activation(
+                out=norm[:, a : a + 1], in_=sum_sq[:, a : a + 1], func=FUNC.Sqrt, bias=EPS * H
+            )
+            nc.vector.reciprocal(out=inv_norm[:, a : a + 1], in_=norm[:, a : a + 1])
+            nc.vector.scalar_tensor_tensor(
+                out=out_sb[:, a, :].rearrange("r (p t) -> r p t", t=CHANNEL_TILES),
+                in0=y[:].rearrange("r (t p) -> r p t", t=CHANNEL_TILES),
+                scalar=inv_norm[:, a : a + 1],
+                in1=gain[:].rearrange("r (p t) -> r p t", t=CHANNEL_TILES),
+                op0=MULT,
+                op1=MULT,
+            )
+            nc.sync.dma_start(out=out_dram[:, a, :], in_=out_sb[:, a, :])

@@ -51,7 +51,6 @@ def tile_conv2dlinalgrmsnorm_s_kernel(tc, hidden_states, conv_w, norm_w, out):
         nc.vector.memset(warm[:], 1.0)
         nc.scalar.activation(out=warm[:], in_=warm[:], func=FUNC.Sqrt)
 
-        nc.scalar.dma_start(out=gain_row[0:1, :], in_=norm_w.unsqueeze(0))
         w_sb = []
         x_sb = keep.tile([P, TOKEN_TILES, H], BF16)
         for l in range(LAYERS):
@@ -60,13 +59,16 @@ def tile_conv2dlinalgrmsnorm_s_kernel(tc, hidden_states, conv_w, norm_w, out):
             w_sb.append(w_l)
             if l == X_BEHIND_LAYER:
                 nc.sync.dma_start(out=x_sb[:], in_=x_dram)
+                nc.sync.dma_start(out=gain_row[0:1, :], in_=norm_w.unsqueeze(0))
 
-        gain_ps = banks.tile([P, CHANNELS], F32, tag="bank")
-        nc.tensor.matmul(out=gain_ps[:], lhsT=ones[:], rhs=gain_row[:], start=True, stop=True)
         gain = keep.tile([P, CHANNELS], F32)
-        nc.scalar.activation(
-            out=gain[:], in_=gain_ps[:], func=FUNC.Copy, scale=math.sqrt(H) / LAYERS
-        )
+
+        def spread_gain():
+            gain_ps = banks.tile([P, CHANNELS], F32, tag="bank")
+            nc.tensor.matmul(out=gain_ps[:], lhsT=ones[:], rhs=gain_row[:], start=True, stop=True)
+            nc.scalar.activation(
+                out=gain[:], in_=gain_ps[:], func=FUNC.Copy, scale=math.sqrt(H) / LAYERS
+            )
 
         def transposed_layer(l):
             w_t = banks.tile([P, CHANNEL_TILES, HALVES, P], F32, tag="bank")
@@ -118,6 +120,7 @@ def tile_conv2dlinalgrmsnorm_s_kernel(tc, hidden_states, conv_w, norm_w, out):
                         out=x_grouped_words[:, a0 : a0 + 2],
                         in_=x_t[:].rearrange("q a u r -> q a r u"),
                     )
+                spread_gain()
             if l == X_QUANTISED_BEHIND_LAYER:
                 nc.vector.quantize_mx(
                     out=x_codes[:].bitcast(FP8X4),

@@ -24,6 +24,9 @@ HALVES = 2
 PAIR = 2
 PACK = HALVES * PAIR
 
+GPSIMD_COLUMNS = 76
+SPLIT = P - GPSIMD_COLUMNS
+
 X_BEHIND_LAYER = 2
 X_QUANTISED_BEHIND_LAYER = 4
 
@@ -39,6 +42,7 @@ def tile_conv2dlinalgrmsnorm_s_kernel(tc, hidden_states, conv_w, norm_w, out):
     with (
         tc.tile_pool(name="keep", bufs=1) as keep,
         tc.tile_pool(name="layers", bufs=LAYERS) as layers,
+        tc.tile_pool(name="stage", bufs=4) as stage,
         tc.psum_pool(name="banks", bufs=8) as banks,
     ):
         ident = keep.tile([P, P], F32)
@@ -61,7 +65,28 @@ def tile_conv2dlinalgrmsnorm_s_kernel(tc, hidden_states, conv_w, norm_w, out):
                 nc.sync.dma_start(out=x_sb[:], in_=x_dram)
                 nc.sync.dma_start(out=gain_row[0:1, :], in_=norm_w.unsqueeze(0))
 
+        x_grouped = keep.tile([P, TOKEN_TILES, P, PACK], BF16, align_bytes=64)
+        x_codes = keep.tile([P, TOKENS], U32, align_bytes=64)
+        x_scales = keep.tile([P, TOKENS], U8, align_bytes=64)
+        w_grouped = keep.tile([P, CHANNEL_TILES, P, PACK], BF16, align_bytes=64)
+        w_codes = keep.tile([P, CHANNELS], U32, align_bytes=64)
+        w_scales = keep.tile([P, CHANNELS], U8, align_bytes=64)
         gain = keep.tile([P, CHANNELS], F32)
+
+        def transpose_x():
+            x_words = x_sb[:].bitcast(F32)
+            x_grouped_words = x_grouped[:].bitcast(F32)
+            for a0 in range(0, TOKEN_TILES, 2):
+                x_t = banks.tile([P, 2, HALVES, P], F32, tag="bank")
+                for a in range(2):
+                    for u in range(HALVES):
+                        nc.tensor.transpose(
+                            x_t[:, a, u, :], x_words[:, a0 + a, u * P : (u + 1) * P], ident[:]
+                        )
+                nc.scalar.copy(
+                    out=x_grouped_words[:, a0 : a0 + 2],
+                    in_=x_t[:].rearrange("q a u r -> q a r u"),
+                )
 
         def spread_gain():
             gain_ps = banks.tile([P, CHANNELS], F32, tag="bank")
@@ -70,56 +95,40 @@ def tile_conv2dlinalgrmsnorm_s_kernel(tc, hidden_states, conv_w, norm_w, out):
                 out=gain[:], in_=gain_ps[:], func=FUNC.Copy, scale=math.sqrt(H) / LAYERS
             )
 
-        def transposed_layer(l):
+        def add_layer(engine, l, acc, values, grouped):
+            if l < LAYERS - 1:
+                engine.tensor_tensor(out=acc, in0=values, in1=acc, op=ADD)
+            else:
+                engine.tensor_tensor(
+                    out=grouped.rearrange("q p (u e) -> q p u e", e=PAIR),
+                    in0=values.rearrange("q u (p e) -> q p u e", e=PAIR),
+                    in1=acc.rearrange("q u (p e) -> q p u e", e=PAIR),
+                    op=ADD,
+                )
+
+        acc_0 = keep.tile([P, HALVES, P * PAIR], F32)
+        acc_1 = keep.tile([P, HALVES, SPLIT * PAIR], F32)
+        acc_g = keep.tile([P, HALVES, GPSIMD_COLUMNS * PAIR], F32)
+        for l in range(LAYERS):
             w_t = banks.tile([P, CHANNEL_TILES, HALVES, P], F32, tag="bank")
-            words = w_sb[l][:].bitcast(F32)
+            w_words = w_sb[l][:].bitcast(F32)
             for t in range(CHANNEL_TILES):
                 for u in range(HALVES):
-                    nc.tensor.transpose(w_t[:, t, u, :], words[:, t, u * P : (u + 1) * P], ident[:])
-            return w_t
-
-        w_acc = keep.tile([P, CHANNEL_TILES, HALVES * P * PAIR], F32)
-        w_grouped = keep.tile([P, CHANNEL_TILES, P, PACK], BF16, align_bytes=64)
-        x_grouped = keep.tile([P, TOKEN_TILES, P, PACK], BF16, align_bytes=64)
-        x_codes = keep.tile([P, TOKENS], U32, align_bytes=64)
-        x_scales = keep.tile([P, TOKENS], U8, align_bytes=64)
-        w_codes = keep.tile([P, CHANNELS], U32, align_bytes=64)
-        w_scales = keep.tile([P, CHANNELS], U8, align_bytes=64)
-
-        for l in range(LAYERS):
-            w_t = transposed_layer(l)
-            for t in range(CHANNEL_TILES):
-                values = w_t[:, t].bitcast(BF16)
-                if l == 0:
-                    nc.scalar.copy(out=w_acc[:, t, :], in_=values.rearrange("q u c -> q (u c)"))
-                elif l < LAYERS - 1:
-                    nc.vector.tensor_tensor(
-                        out=w_acc[:, t, :],
-                        in0=values.rearrange("q u c -> q (u c)"),
-                        in1=w_acc[:, t, :],
-                        op=ADD,
-                    )
-                else:
-                    nc.vector.tensor_tensor(
-                        out=w_grouped[:, t].rearrange("q p (u e) -> q p u e", e=PAIR),
-                        in0=values.rearrange("q u (p e) -> q p u e", e=PAIR),
-                        in1=w_acc[:, t, :].rearrange("q (u p e) -> q p u e", u=HALVES, e=PAIR),
-                        op=ADD,
-                    )
+                    nc.tensor.transpose(w_t[:, t, u, :], w_words[:, t, u * P : (u + 1) * P], ident[:])
+            values_0 = w_t[:, 0].bitcast(BF16)
+            values_1 = w_t[:, 1, :, 0:SPLIT].bitcast(BF16)
+            if l == 0:
+                nc.scalar.copy(out=acc_g[:], in_=w_t[:, 1, :, SPLIT:P].bitcast(BF16))
+                nc.scalar.copy(out=acc_0[:], in_=values_0)
+                nc.scalar.copy(out=acc_1[:], in_=values_1)
+            else:
+                words_g = stage.tile([P, HALVES, GPSIMD_COLUMNS], F32)
+                nc.scalar.copy(out=words_g[:], in_=w_t[:, 1, :, SPLIT:P])
+                add_layer(nc.vector, l, acc_0[:], values_0, w_grouped[:, 0])
+                add_layer(nc.vector, l, acc_1[:], values_1, w_grouped[:, 1, 0:SPLIT])
+                add_layer(nc.gpsimd, l, acc_g[:], words_g[:].bitcast(BF16), w_grouped[:, 1, SPLIT:P])
             if l == X_BEHIND_LAYER:
-                x_words = x_sb[:].bitcast(F32)
-                x_grouped_words = x_grouped[:].bitcast(F32)
-                for a0 in range(0, TOKEN_TILES, 2):
-                    x_t = banks.tile([P, 2, HALVES, P], F32, tag="bank")
-                    for a in range(2):
-                        for u in range(HALVES):
-                            nc.tensor.transpose(
-                                x_t[:, a, u, :], x_words[:, a0 + a, u * P : (u + 1) * P], ident[:]
-                            )
-                    nc.scalar.copy(
-                        out=x_grouped_words[:, a0 : a0 + 2],
-                        in_=x_t[:].rearrange("q a u r -> q a r u"),
-                    )
+                transpose_x()
                 spread_gain()
             if l == X_QUANTISED_BEHIND_LAYER:
                 nc.vector.quantize_mx(

@@ -24,11 +24,11 @@ HALVES = 2
 PAIR = 2
 PACK = HALVES * PAIR
 
-GPSIMD_COLUMNS = 76
+GPSIMD_COLUMNS = 72
 SPLIT = P - GPSIMD_COLUMNS
 
-X_BEHIND_LAYER = 2
-X_QUANTISED_BEHIND_LAYER = 4
+X_BEHIND_LAYER = 6
+X_QUANTISED_BEHIND_LAYER = 8
 
 FLOPS = 2 * TOKENS * H * CHANNELS
 
@@ -109,24 +109,29 @@ def tile_conv2dlinalgrmsnorm_s_kernel(tc, hidden_states, conv_w, norm_w, out):
         acc_0 = keep.tile([P, HALVES, P * PAIR], F32)
         acc_1 = keep.tile([P, HALVES, SPLIT * PAIR], F32)
         acc_g = keep.tile([P, HALVES, GPSIMD_COLUMNS * PAIR], F32)
-        for l in range(LAYERS):
-            w_t = banks.tile([P, CHANNEL_TILES, HALVES, P], F32, tag="bank")
+
+        def transposed(l, t):
+            w_t = banks.tile([P, HALVES, P], F32, tag="bank")
             w_words = w_sb[l][:].bitcast(F32)
-            for t in range(CHANNEL_TILES):
-                for u in range(HALVES):
-                    nc.tensor.transpose(w_t[:, t, u, :], w_words[:, t, u * P : (u + 1) * P], ident[:])
-            values_0 = w_t[:, 0].bitcast(BF16)
-            values_1 = w_t[:, 1, :, 0:SPLIT].bitcast(BF16)
+            for u in range(HALVES):
+                nc.tensor.transpose(w_t[:, u, :], w_words[:, t, u * P : (u + 1) * P], ident[:])
+            return w_t
+
+        for l in range(LAYERS):
+            w_t1 = transposed(l, 1)
+            w_t0 = transposed(l, 0)
+            values_0 = w_t0[:].bitcast(BF16)
+            values_1 = w_t1[:, :, 0:SPLIT].bitcast(BF16)
             if l == 0:
-                nc.scalar.copy(out=acc_g[:], in_=w_t[:, 1, :, SPLIT:P].bitcast(BF16))
-                nc.scalar.copy(out=acc_0[:], in_=values_0)
+                nc.scalar.copy(out=acc_g[:], in_=w_t1[:, :, SPLIT:P].bitcast(BF16))
                 nc.scalar.copy(out=acc_1[:], in_=values_1)
+                nc.vector.tensor_copy(out=acc_0[:], in_=values_0)
             else:
                 words_g = stage.tile([P, HALVES, GPSIMD_COLUMNS], F32)
-                nc.scalar.copy(out=words_g[:], in_=w_t[:, 1, :, SPLIT:P])
+                nc.scalar.copy(out=words_g[:], in_=w_t1[:, :, SPLIT:P])
+                add_layer(nc.gpsimd, l, acc_g[:], words_g[:].bitcast(BF16), w_grouped[:, 1, SPLIT:P])
                 add_layer(nc.vector, l, acc_0[:], values_0, w_grouped[:, 0])
                 add_layer(nc.vector, l, acc_1[:], values_1, w_grouped[:, 1, 0:SPLIT])
-                add_layer(nc.gpsimd, l, acc_g[:], words_g[:].bitcast(BF16), w_grouped[:, 1, SPLIT:P])
             if l == X_BEHIND_LAYER:
                 transpose_x()
                 spread_gain()

@@ -24,7 +24,7 @@ HALVES = 2
 PAIR = 2
 PACK = HALVES * PAIR
 
-GPSIMD_COLUMNS = 72
+GPSIMD_COLUMNS = 80
 SPLIT = P - GPSIMD_COLUMNS
 
 X_BEHIND_LAYER = 6
@@ -53,7 +53,7 @@ def tile_conv2dlinalgrmsnorm_s_kernel(tc, hidden_states, conv_w, norm_w, out):
         nc.vector.memset(gain_row[:], 0.0)
         warm = keep.tile([P, 1], F32)
         nc.vector.memset(warm[:], 1.0)
-        nc.scalar.activation(out=warm[:], in_=warm[:], func=FUNC.Sqrt)
+        nc.scalar.activation(out=warm[:], in_=warm[:], func=FUNC.Abs_reciprocal_sqrt)
 
         w_sb = []
         x_sb = keep.tile([P, TOKEN_TILES, H], BF16)
@@ -150,7 +150,6 @@ def tile_conv2dlinalgrmsnorm_s_kernel(tc, hidden_states, conv_w, norm_w, out):
 
         squares = keep.tile([P, CHANNELS], F32)
         sum_sq = keep.tile([P, TOKEN_TILES], F32)
-        norm = keep.tile([P, TOKEN_TILES], F32)
         inv_norm = keep.tile([P, TOKEN_TILES], F32)
         out_sb = keep.tile([P, TOKEN_TILES, CHANNELS], F32)
         for a in range(TOKEN_TILES):
@@ -173,9 +172,11 @@ def tile_conv2dlinalgrmsnorm_s_kernel(tc, hidden_states, conv_w, norm_w, out):
                 accum_out=sum_sq[:, a : a + 1],
             )
             nc.scalar.activation(
-                out=norm[:, a : a + 1], in_=sum_sq[:, a : a + 1], func=FUNC.Sqrt, bias=EPS * H
+                out=inv_norm[:, a : a + 1],
+                in_=sum_sq[:, a : a + 1],
+                func=FUNC.Abs_reciprocal_sqrt,
+                bias=EPS * H,
             )
-            nc.vector.reciprocal(out=inv_norm[:, a : a + 1], in_=norm[:, a : a + 1])
             nc.vector.scalar_tensor_tensor(
                 out=out_sb[:, a, :].rearrange("r (p t) -> r p t", t=CHANNEL_TILES),
                 in0=y[:].rearrange("r (t p) -> r p t", t=CHANNEL_TILES),

@@ -24,11 +24,10 @@ HALVES = 2
 PAIR = 2
 PACK = HALVES * PAIR
 
-GPSIMD_COLUMNS = 80
+GPSIMD_COLUMNS = 60
 SPLIT = P - GPSIMD_COLUMNS
 
-X_BEHIND_LAYER = 6
-X_QUANTISED_BEHIND_LAYER = 8
+X_BEHIND_LAYER = 7
 
 FLOPS = 2 * TOKENS * H * CHANNELS
 
@@ -36,14 +35,15 @@ FLOPS = 2 * TOKENS * H * CHANNELS
 def tile_conv2dlinalgrmsnorm_s_kernel(tc, hidden_states, conv_w, norm_w, out):
     nc = tc.nc
     x_dram = hidden_states.flatten_outer_dims().rearrange("(p a) h -> p a h", a=TOKEN_TILES)
-    w_dram = conv_w.rearrange("l (p t) h -> l p t h", t=CHANNEL_TILES)
+    w_dram = conv_w.rearrange("l (p t) h -> l t p h", t=CHANNEL_TILES)
     out_dram = out.flatten_outer_dims().rearrange("(p a) c -> p a c", a=TOKEN_TILES)
 
     with (
         tc.tile_pool(name="keep", bufs=1) as keep,
-        tc.tile_pool(name="layers", bufs=LAYERS) as layers,
+        tc.tile_pool(name="layers", bufs=LAYERS * CHANNEL_TILES) as layers,
         tc.tile_pool(name="stage", bufs=4) as stage,
         tc.psum_pool(name="banks", bufs=8) as banks,
+        tc.manual_schedule(),
     ):
         ident = keep.tile([P, P], F32)
         make_identity(nc, ident[:])
@@ -55,13 +55,15 @@ def tile_conv2dlinalgrmsnorm_s_kernel(tc, hidden_states, conv_w, norm_w, out):
         nc.vector.memset(warm[:], 1.0)
         nc.scalar.activation(out=warm[:], in_=warm[:], func=FUNC.Abs_reciprocal_sqrt)
 
-        w_sb = []
+        w_sb = {}
         x_sb = keep.tile([P, TOKEN_TILES, H], BF16)
-        for l in range(LAYERS):
-            w_l = layers.tile([P, CHANNEL_TILES, H], BF16, tag="w")
-            nc.sync.dma_start(out=w_l[:], in_=w_dram[l])
-            w_sb.append(w_l)
-            if l == X_BEHIND_LAYER:
+        for l0 in range(0, LAYERS, 2):
+            for t in range(CHANNEL_TILES):
+                for l in (l0, l0 + 1):
+                    w_lt = layers.tile([P, H], BF16, tag="w")
+                    nc.sync.dma_start(out=w_lt[:], in_=w_dram[l, t])
+                    w_sb[l, t] = w_lt
+            if l0 + 1 == X_BEHIND_LAYER:
                 nc.sync.dma_start(out=x_sb[:], in_=x_dram)
                 nc.sync.dma_start(out=gain_row[0:1, :], in_=norm_w.unsqueeze(0))
 
@@ -112,36 +114,40 @@ def tile_conv2dlinalgrmsnorm_s_kernel(tc, hidden_states, conv_w, norm_w, out):
 
         def transposed(l, t):
             w_t = banks.tile([P, HALVES, P], F32, tag="bank")
-            w_words = w_sb[l][:].bitcast(F32)
+            w_words = w_sb[l, t][:].bitcast(F32)
             for u in range(HALVES):
-                nc.tensor.transpose(w_t[:, u, :], w_words[:, t, u * P : (u + 1) * P], ident[:])
+                nc.tensor.transpose(w_t[:, u, :], w_words[:, u * P : (u + 1) * P], ident[:])
             return w_t
 
-        for l in range(LAYERS):
-            w_t1 = transposed(l, 1)
-            w_t0 = transposed(l, 0)
-            values_0 = w_t0[:].bitcast(BF16)
-            values_1 = w_t1[:, :, 0:SPLIT].bitcast(BF16)
-            if l == 0:
-                nc.scalar.copy(out=acc_g[:], in_=w_t1[:, :, SPLIT:P].bitcast(BF16))
-                nc.scalar.copy(out=acc_1[:], in_=values_1)
-                nc.vector.tensor_copy(out=acc_0[:], in_=values_0)
-            else:
-                words_g = stage.tile([P, HALVES, GPSIMD_COLUMNS], F32)
-                nc.scalar.copy(out=words_g[:], in_=w_t1[:, :, SPLIT:P])
-                add_layer(nc.gpsimd, l, acc_g[:], words_g[:].bitcast(BF16), w_grouped[:, 1, SPLIT:P])
-                add_layer(nc.vector, l, acc_0[:], values_0, w_grouped[:, 0])
-                add_layer(nc.vector, l, acc_1[:], values_1, w_grouped[:, 1, 0:SPLIT])
-            if l == X_BEHIND_LAYER:
+        for l0 in range(0, LAYERS, 2):
+            w_t = {}
+            for t in range(CHANNEL_TILES):
+                for l in (l0, l0 + 1):
+                    w_t[l, t] = transposed(l, t)
+            for l in (l0, l0 + 1):
+                values_0 = w_t[l, 0][:].bitcast(BF16)
+                values_1 = w_t[l, 1][:, :, 0:SPLIT].bitcast(BF16)
+                if l == 0:
+                    nc.vector.tensor_copy(out=acc_0[:], in_=values_0)
+                    nc.scalar.copy(out=acc_g[:], in_=w_t[l, 1][:, :, SPLIT:P].bitcast(BF16))
+                    nc.scalar.copy(out=acc_1[:], in_=values_1)
+                else:
+                    words_g = stage.tile([P, HALVES, GPSIMD_COLUMNS], F32)
+                    nc.scalar.copy(out=words_g[:], in_=w_t[l, 1][:, :, SPLIT:P])
+                    add_layer(
+                        nc.gpsimd, l, acc_g[:], words_g[:].bitcast(BF16), w_grouped[:, 1, SPLIT:P]
+                    )
+                    add_layer(nc.vector, l, acc_0[:], values_0, w_grouped[:, 0])
+                    add_layer(nc.vector, l, acc_1[:], values_1, w_grouped[:, 1, 0:SPLIT])
+            if l0 + 1 == X_BEHIND_LAYER:
                 transpose_x()
                 spread_gain()
-            if l == X_QUANTISED_BEHIND_LAYER:
-                nc.vector.quantize_mx(
-                    out=x_codes[:].bitcast(FP8X4),
-                    scales=x_scales[:],
-                    in_=x_grouped[:].rearrange("q a r k -> q (a r k)"),
-                )
 
+        nc.vector.quantize_mx(
+            out=x_codes[:].bitcast(FP8X4),
+            scales=x_scales[:],
+            in_=x_grouped[:].rearrange("q a r k -> q (a r k)"),
+        )
         nc.vector.quantize_mx(
             out=w_codes[:].bitcast(FP8X4),
             scales=w_scales[:],

import math

import concourse.mybir as mybir
from concourse.masks import make_identity

BF16 = mybir.dt.bfloat16
F32 = mybir.dt.float32
U32 = mybir.dt.uint32
U8 = mybir.dt.uint8
FP8X4 = mybir.dt.float8_e4m3fn_x4
ADD = mybir.AluOpType.add
MULT = mybir.AluOpType.mult
FUNC = mybir.ActivationFunctionType

P = 128
TOKENS = 512
H = 512
CHANNELS = 256
LAYERS = 10
EPS = 1e-06
TOKEN_TILES = TOKENS // P
CHANNEL_TILES = CHANNELS // P
HALVES = 2
PAIR = 2
PACK = HALVES * PAIR

GPSIMD_COLUMNS = 60
SPLIT = P - GPSIMD_COLUMNS

X_BEHIND_LAYER = 7

FLOPS = 2 * TOKENS * H * CHANNELS


def tile_conv2dlinalgrmsnorm_s_kernel(tc, hidden_states, conv_w, norm_w, out):
    nc = tc.nc
    x_dram = hidden_states.flatten_outer_dims().rearrange("(p a) h -> p a h", a=TOKEN_TILES)
    w_dram = conv_w.rearrange("l (p t) h -> l t p h", t=CHANNEL_TILES)
    out_dram = out.flatten_outer_dims().rearrange("(p a) c -> p a c", a=TOKEN_TILES)

    with (
        tc.tile_pool(name="keep", bufs=1) as keep,
        tc.tile_pool(name="layers", bufs=LAYERS * CHANNEL_TILES) as layers,
        tc.tile_pool(name="stage", bufs=4) as stage,
        tc.psum_pool(name="banks", bufs=8) as banks,
        tc.manual_schedule(),
    ):
        ident = keep.tile([P, P], F32)
        make_identity(nc, ident[:])
        ones = keep.tile([P, P], BF16)
        nc.vector.memset(ones[:], 1.0)
        gain_row = keep.tile([P, CHANNELS], BF16)
        nc.vector.memset(gain_row[:], 0.0)
        warm = keep.tile([P, 1], F32)
        nc.vector.memset(warm[:], 1.0)
        nc.scalar.activation(out=warm[:], in_=warm[:], func=FUNC.Abs_reciprocal_sqrt)

        w_sb = {}
        x_sb = keep.tile([P, TOKEN_TILES, H], BF16)
        for l0 in range(0, LAYERS, 2):
            for t in range(CHANNEL_TILES):
                for l in (l0, l0 + 1):
                    w_lt = layers.tile([P, H], BF16, tag="w")
                    nc.sync.dma_start(out=w_lt[:], in_=w_dram[l, t])
                    w_sb[l, t] = w_lt
            if l0 + 1 == X_BEHIND_LAYER:
                nc.sync.dma_start(out=x_sb[:], in_=x_dram)
                nc.sync.dma_start(out=gain_row[0:1, :], in_=norm_w.unsqueeze(0))

        x_grouped = keep.tile([P, TOKEN_TILES, P, PACK], BF16, align_bytes=64)
        x_codes = keep.tile([P, TOKENS], U32, align_bytes=64)
        x_scales = keep.tile([P, TOKENS], U8, align_bytes=64)
        w_grouped = keep.tile([P, CHANNEL_TILES, P, PACK], BF16, align_bytes=64)
        w_codes = keep.tile([P, CHANNELS], U32, align_bytes=64)
        w_scales = keep.tile([P, CHANNELS], U8, align_bytes=64)
        gain = keep.tile([P, CHANNELS], F32)

        def transpose_x():
            x_words = x_sb[:].bitcast(F32)
            x_grouped_words = x_grouped[:].bitcast(F32)
            for a0 in range(0, TOKEN_TILES, 2):
                x_t = banks.tile([P, 2, HALVES, P], F32, tag="bank")
                for a in range(2):
                    for u in range(HALVES):
                        nc.tensor.transpose(
                            x_t[:, a, u, :], x_words[:, a0 + a, u * P : (u + 1) * P], ident[:]
                        )
                nc.scalar.copy(
                    out=x_grouped_words[:, a0 : a0 + 2],
                    in_=x_t[:].rearrange("q a u r -> q a r u"),
                )

        def spread_gain():
            gain_ps = banks.tile([P, CHANNELS], F32, tag="bank")
            nc.tensor.matmul(out=gain_ps[:], lhsT=ones[:], rhs=gain_row[:], start=True, stop=True)
            nc.scalar.activation(
                out=gain[:], in_=gain_ps[:], func=FUNC.Copy, scale=math.sqrt(H) / LAYERS
            )

        def add_layer(engine, l, acc, values, grouped):
            if l < LAYERS - 1:
                engine.tensor_tensor(out=acc, in0=values, in1=acc, op=ADD)
            else:
                engine.tensor_tensor(
                    out=grouped.rearrange("q p (u e) -> q p u e", e=PAIR),
                    in0=values.rearrange("q u (p e) -> q p u e", e=PAIR),
                    in1=acc.rearrange("q u (p e) -> q p u e", e=PAIR),
                    op=ADD,
                )

        acc_0 = keep.tile([P, HALVES, P * PAIR], F32)
        acc_1 = keep.tile([P, HALVES, SPLIT * PAIR], F32)
        acc_g = keep.tile([P, HALVES, GPSIMD_COLUMNS * PAIR], F32)

        def transposed(l, t):
            w_t = banks.tile([P, HALVES, P], F32, tag="bank")
            w_words = w_sb[l, t][:].bitcast(F32)
            for u in range(HALVES):
                nc.tensor.transpose(w_t[:, u, :], w_words[:, u * P : (u + 1) * P], ident[:])
            return w_t

        for l0 in range(0, LAYERS, 2):
            w_t = {}
            for t in range(CHANNEL_TILES):
                for l in (l0, l0 + 1):
                    w_t[l, t] = transposed(l, t)
            for l in (l0, l0 + 1):
                values_0 = w_t[l, 0][:].bitcast(BF16)
                values_1 = w_t[l, 1][:, :, 0:SPLIT].bitcast(BF16)
                if l == 0:
                    nc.vector.tensor_copy(out=acc_0[:], in_=values_0)
                    nc.scalar.copy(out=acc_g[:], in_=w_t[l, 1][:, :, SPLIT:P].bitcast(BF16))
                    nc.scalar.copy(out=acc_1[:], in_=values_1)
                else:
                    words_g = stage.tile([P, HALVES, GPSIMD_COLUMNS], F32)
                    nc.scalar.copy(out=words_g[:], in_=w_t[l, 1][:, :, SPLIT:P])
                    add_layer(
                        nc.gpsimd, l, acc_g[:], words_g[:].bitcast(BF16), w_grouped[:, 1, SPLIT:P]
                    )
                    add_layer(nc.vector, l, acc_0[:], values_0, w_grouped[:, 0])
                    add_layer(nc.vector, l, acc_1[:], values_1, w_grouped[:, 1, 0:SPLIT])
            if l0 + 1 == X_BEHIND_LAYER:
                transpose_x()
                spread_gain()

        nc.vector.quantize_mx(
            out=x_codes[:].bitcast(FP8X4),
            scales=x_scales[:],
            in_=x_grouped[:].rearrange("q a r k -> q (a r k)"),
        )
        nc.vector.quantize_mx(
            out=w_codes[:].bitcast(FP8X4),
            scales=w_scales[:],
            in_=w_grouped[:].rearrange("q t p k -> q (t p k)"),
        )

        squares = keep.tile([P, CHANNELS], F32)
        sum_sq = keep.tile([P, TOKEN_TILES], F32)
        inv_norm = keep.tile([P, TOKEN_TILES], F32)
        out_sb = keep.tile([P, TOKEN_TILES, CHANNELS], F32)
        for a in range(TOKEN_TILES):
            rows = slice(a * P, (a + 1) * P)
            y = banks.tile([P, CHANNELS], F32, tag="bank")
            nc.tensor.matmul_mx(
                out=y[:],
                lhsT=x_codes[:, rows].bitcast(FP8X4),
                lhsT_scale=x_scales[:, rows],
                rhs=w_codes[:].bitcast(FP8X4),
                rhs_scale=w_scales[:],
                start=True,
                stop=True,
            )
            nc.scalar.activation(
                out=squares[:],
                in_=y[:],
                func=FUNC.Square,
                scale=1.0 / LAYERS,
                accum_out=sum_sq[:, a : a + 1],
            )
            nc.scalar.activation(
                out=inv_norm[:, a : a + 1],
                in_=sum_sq[:, a : a + 1],
                func=FUNC.Abs_reciprocal_sqrt,
                bias=EPS * H,
            )
            nc.vector.scalar_tensor_tensor(
                out=out_sb[:, a, :].rearrange("r (p t) -> r p t", t=CHANNEL_TILES),
                in0=y[:].rearrange("r (t p) -> r p t", t=CHANNEL_TILES),
                scalar=inv_norm[:, a : a + 1],
                in1=gain[:].rearrange("r (p t) -> r p t", t=CHANNEL_TILES),
                op0=MULT,
                op1=MULT,
            )
            nc.sync.dma_start(out=out_dram[:, a, :], in_=out_sb[:, a, :])
